import numpy as np
import ml_dtypes


def mxq(x, axis, fmt="e4m3"):
    dtype, down = {"e4m3": (ml_dtypes.float8_e4m3fn, 7), "e5m2": (ml_dtypes.float8_e5m2, 14)}[fmt]
    v = np.moveaxis(np.asarray(x, np.float32).astype(ml_dtypes.bfloat16).astype(np.float64), axis, -1)
    blocks = v.reshape(v.shape[:-1] + (-1, 32))
    amax = np.abs(blocks).max(-1, keepdims=True)
    byte = np.maximum(np.where(amax > 0, np.frexp(amax)[1] - 1 + 127, 0) - down, 1)
    scale = np.exp2(byte - 127.0)
    codes = (blocks / scale).astype(np.float32).astype(dtype).astype(np.float64)
    return np.moveaxis((codes * scale).reshape(v.shape), -1, axis)


WIDE = False


def mx_kscale(k):
    if not WIDE:
        return np.ones(k)
    levels = np.array([10, -10, 5, -5, 0])
    a = np.random.permutation(np.resize(levels, k // 512 * 4)).reshape(k // 512, 4)
    idx = np.arange(k)
    return np.exp2(a[idx // 512, idx % 128 // 32])


BF16 = ml_dtypes.bfloat16


def bf(x):
    return np.asarray(x, np.float32).astype(BF16)


def f64(x):
    return np.asarray(x).astype(np.float64)


B, N, D, F, M1, M2 = 4, 1024, 512, 256, 3, 5
D2 = D + D


def silu(v):
    return v / (1.0 + np.exp(-v))


def setup_inputs():
    s, t = mx_kscale(D), mx_kscale(D2)
    return {"h": bf(np.random.standard_normal((B, N, D)) * t[:D]),
            "x1": bf(np.random.standard_normal((B, N, D, M1)) * s[:, None]),
            "pre1": bf(np.random.standard_normal((D, D)) / np.sqrt(D) / s[:, None] * t[D:]),
            "w1_0": bf(np.random.standard_normal((D2, F)) / np.sqrt(D2) / t[:, None]),
            "b1_0": bf(np.random.standard_normal(F) * 0.2)}


def reference(h, x1, pre1, w1_0, b1_0):
    xt = f64(x1).swapaxes(-1, -2).reshape(B * N * M1, D)
    pm = (mxq(xt, 1, "e4m3") @ mxq(f64(pre1), 0, "e4m3")).reshape(B, N, M1, D)
    inv = np.sqrt(np.sum(pm * pm, axis=-2))
    mlp_in = np.concatenate([f64(h), inv], axis=-1)
    return silu((mxq(mlp_in, 2, "e4m3") @ mxq(f64(w1_0), 0, "e4m3")) + f64(b1_0))

@@ -1,0 +1,290 @@
+from contextlib import ExitStack
+
+import concourse.mybir as mybir
+from concourse.masks import make_identity
+
+FLOPS = 2 * 12288 * 512 * 512 + 2 * 4096 * 1024 * 256
+
+BF16 = mybir.dt.bfloat16
+F32 = mybir.dt.float32
+U32 = mybir.dt.uint32
+U8 = mybir.dt.uint8
+FP8X4 = mybir.dt.float8_e4m3fn_x4
+AF = mybir.ActivationFunctionType
+ALU = mybir.AluOpType
+
+P = 128
+NB = 16
+BT = 256
+
+
+def tile_equivariantfeedforward_pa_t_kernel(tc, h, x1, pre1, w1_0, b1_0, out):
+    nc = tc.nc
+
+    xv = x1.rearrange("b n (j d) m -> (b n j) (d m)", j=2).rearrange("(g p) c -> p g c", p=P)
+    hv = h.rearrange("b n k -> (b n) k").rearrange("(i p) k -> p i k", p=P)
+    ov = out.rearrange("b n f -> (b n) f").rearrange("(i p) f -> p i f", p=P)
+
+    with ExitStack() as ctx:
+        const = ctx.enter_context(tc.tile_pool(name="const", bufs=1))
+        xpool = ctx.enter_context(tc.tile_pool(name="xpool", bufs=4))
+        gpool = ctx.enter_context(tc.tile_pool(name="gpool", bufs=2))
+        cpool = ctx.enter_context(tc.tile_pool(name="cpool", bufs=5))
+        spool = ctx.enter_context(tc.tile_pool(name="spool", bufs=6))
+        apool = ctx.enter_context(tc.tile_pool(name="apool", bufs=2))
+        ipool = ctx.enter_context(tc.tile_pool(name="ipool", bufs=3))
+        vpool = ctx.enter_context(tc.tile_pool(name="vpool", bufs=8))
+        ps_tp = ctx.enter_context(tc.psum_pool(name="ps_tp", bufs=3))
+        ps_pm = ctx.enter_context(tc.psum_pool(name="ps_pm", bufs=4))
+        ps_ob = ctx.enter_context(tc.psum_pool(name="ps_ob", bufs=1))
+        ctx.enter_context(tc.manual_schedule())
+
+        xs_t, hs_t, tp_t, xg_t, cod_t, scl_t = {}, {}, {}, {}, {}, {}
+        pm_t, s_t, t_t, a_t, ig_t, iq_t, isc_t, ob_t, v_t = {}, {}, {}, {}, {}, {}, {}, {}, {}
+
+        ident_bf = const.tile([P, P], BF16, name="ident_bf")
+        ident_f = const.tile([P, P], F32, name="ident_f")
+        make_identity(nc, ident_bf[:])
+        make_identity(nc, ident_f[:])
+
+        one = const.tile([P, 1], F32, name="one")
+        one_s = const.tile([P, 1], F32, name="one_s")
+        nc.vector.memset(one[:], 1.0)
+
+        pw = const.tile([P, 4, 512], BF16, name="pw")
+        pre_v = pre1.rearrange("(j u p) e -> u p j e", j=2, u=2)
+        for u in range(2):
+            nc.scalar.dma_start(out=pw[:, 2 * u : 2 * u + 2, :], in_=pre_v[u])
+        wr = const.tile([P, 2, 4, 256], BF16, name="wr")
+        nc.scalar.dma_start(
+            out=wr[:, 0].rearrange("p (u e) f -> p u (e f)", u=2),
+            in_=w1_0[0:512, :].rearrange("(u p e) f -> p u (e f)", u=2, e=2),
+        )
+        nc.scalar.dma_start(
+            out=wr[:, 1].rearrange("p j f -> p (j f)"),
+            in_=w1_0[512:1024, :].rearrange("(p j) f -> p (j f)", j=4),
+        )
+        bb16 = const.tile([P, 256], BF16, name="bb16")
+        nc.scalar.dma_start(out=bb16[:], in_=b1_0.partition_broadcast(P))
+        nc.scalar.activation(out=one_s[:], in_=one[:], func=AF.Sqrt)
+
+        pg = const.tile([P, 2048], BF16, name="pg", align_bytes=64)
+        pq = const.tile([P, 512], U32, name="pq", align_bytes=64)
+        psc = const.tile([P, 512], U8, name="psc", align_bytes=64)
+        wg = const.tile([P, 2048], BF16, name="wg", align_bytes=64)
+        wq = const.tile([P, 512], U32, name="wq", align_bytes=64)
+        wsc = const.tile([P, 512], U8, name="wsc", align_bytes=64)
+        bias2 = const.tile([P, 2, 256], F32, name="bias2")
+
+        def prep_pre1():
+            nc.vector.tensor_copy(
+                out=pg[:].rearrange("p (j q t) -> p j q t", j=4, t=4),
+                in_=pw[:].rearrange("p t (q j) -> p j q t", j=4),
+            )
+            nc.vector.quantize_mx(out=pq[:].bitcast(FP8X4), scales=psc[:], in_=pg[:])
+
+        def prep_w():
+            nc.vector.tensor_copy(
+                out=wg[:].rearrange("p (s f t) -> p s f t", s=2, t=4),
+                in_=wr[:].rearrange("p s t f -> p s f t"),
+            )
+            nc.vector.quantize_mx(out=wq[:].bitcast(FP8X4), scales=wsc[:], in_=wg[:])
+            for i in range(2):
+                nc.vector.tensor_copy(out=bias2[:, i, :], in_=bb16[:])
+
+        def load(b):
+            hs = xpool.tile([P, 2, 512], BF16, name="hs")
+            nc.sync.dma_start(out=hs[:], in_=hv[:, 2 * b : 2 * b + 2, :])
+            xs = xpool.tile([P, 4, 768], BF16, name="xs")
+            pieces = 2 if b == 0 else 1
+            step = 4 // pieces
+            for g in range(0, 4, step):
+                nc.sync.dma_start(out=xs[:, g : g + step, :], in_=xv[:, 4 * b + g : 4 * b + g + step, :])
+            xs_t[b] = xs
+            hs_t[b] = hs
+
+        def transposes_h(b):
+            th = ps_pm.tile([P, 512], F32, name="pm")
+            hw = hs_t[b][:].bitcast(F32)
+            for i in range(2):
+                for u in range(2):
+                    c = 2 * i + u
+                    nc.tensor.transpose(th[:, c * P : (c + 1) * P], hw[:, i, u * P : (u + 1) * P], ident_f[:])
+            tp_t[(b, 3)] = th
+
+        def transposes_x(b, m):
+            tp = ps_tp.tile([P, 1024], BF16, name="tp")
+            for g in range(4):
+                xg4 = xs_t[b][:, g, :].rearrange("p (u d m) -> p u d m", u=2, m=3)
+                for u in range(2):
+                    c = 2 * g + u
+                    nc.tensor.transpose(tp[:, c * P : (c + 1) * P], xg4[:, u, :, m], ident_bf[:])
+            tp_t[(b, m)] = tp
+
+        def evac(b, k, on_act):
+            if b not in xg_t:
+                xg_t[b] = gpool.tile([P, 4096], BF16, name="xg", align_bytes=64)
+            dst = xg_t[b][:, k * 1024 : (k + 1) * 1024].bitcast(F32)
+            if k < 3:
+                src = tp_t[(b, k)][:].bitcast(F32).rearrange("p (g u a) -> p g a u", g=4, u=2)
+                dst = dst.rearrange("p (g a u) -> p g a u", g=4, u=2)
+            else:
+                src = tp_t[(b, k)][:].rearrange("p (i u t) -> p i t u", i=2, u=2)
+                dst = dst.rearrange("p (i t u) -> p i t u", i=2, u=2)
+            if on_act:
+                nc.scalar.copy(out=dst, in_=src)
+            else:
+                nc.vector.tensor_copy(out=dst, in_=src)
+
+        def quant_block(b):
+            cod = cpool.tile([P, 1024], U32, name="cod", align_bytes=64)
+            scl = cpool.tile([P, 1024], U8, name="scl", align_bytes=64)
+            nc.vector.quantize_mx(out=cod[:].bitcast(FP8X4), scales=scl[:], in_=xg_t[b][:])
+            cod_t[b] = cod
+            scl_t[b] = scl
+
+        def mm1(b, m, jp):
+            pm = ps_pm.tile([P, 512], F32, name="pm")
+            for j2 in range(2):
+                j = 2 * jp + j2
+                nc.tensor.matmul_mx(
+                    out=pm[:, j2 * BT : (j2 + 1) * BT],
+                    lhsT=pq[:, j * P : (j + 1) * P].bitcast(FP8X4),
+                    lhsT_scale=psc[:, j * P : (j + 1) * P],
+                    rhs=cod_t[b][:, m * BT : (m + 1) * BT].bitcast(FP8X4),
+                    rhs_scale=scl_t[b][:, m * BT : (m + 1) * BT],
+                    start=True,
+                    stop=True,
+                )
+            pm_t[(b, m, jp)] = pm
+
+        def square(b, m, jp):
+            if jp == 0:
+                s_t[(b, m)] = spool.tile([P, 1024], F32, name="sq")
+            nc.scalar.activation(out=s_t[(b, m)][:, jp * 512 : (jp + 1) * 512], in_=pm_t[(b, m, jp)][:], func=AF.Square)
+
+        def add1(b):
+            t_t[b] = apool.tile([P, 1024], F32, name="t01")
+            nc.vector.tensor_tensor(out=t_t[b][:], in0=s_t[(b, 0)][:], in1=s_t[(b, 1)][:], op=ALU.add)
+
+        def add2(b):
+            a_t[b] = apool.tile([P, 1024], F32, name="a012")
+            nc.vector.tensor_tensor(
+                out=a_t[b][:].rearrange("p (c t j) -> p c t j", c=2, j=2),
+                in0=t_t[b][:].rearrange("p (c j t) -> p c t j", c=2, j=2),
+                in1=s_t[(b, 2)][:].rearrange("p (c j t) -> p c t j", c=2, j=2),
+                op=ALU.add,
+            )
+
+        def root(b):
+            ig_t[b] = apool.tile([P, 1024], BF16, name="ig", align_bytes=64)
+            nc.scalar.activation(
+                out=ig_t[b][:].rearrange("p (t c j) -> p t c j", c=2, j=2),
+                in_=a_t[b][:].rearrange("p (c t j) -> p t c j", c=2, j=2),
+                func=AF.Sqrt,
+            )
+
+        def quant_inv(b):
+            iq_t[b] = ipool.tile([P, 256], U32, name="iq", align_bytes=64)
+            isc_t[b] = ipool.tile([P, 256], U8, name="isc", align_bytes=64)
+            nc.vector.quantize_mx(out=iq_t[b][:].bitcast(FP8X4), scales=isc_t[b][:], in_=ig_t[b][:])
+
+        def mm2(b):
+            ob = ps_ob.tile([P, 512], F32, name="ob")
+            for i in range(2):
+                o = ob[:, i * 256 : (i + 1) * 256]
+                c0 = 768 + i * P
+                nc.tensor.matmul_mx(
+                    out=o,
+                    lhsT=cod_t[b][:, c0 : c0 + P].bitcast(FP8X4),
+                    lhsT_scale=scl_t[b][:, c0 : c0 + P],
+                    rhs=wq[:, 0:256].bitcast(FP8X4),
+                    rhs_scale=wsc[:, 0:256],
+                    start=True,
+                    stop=False,
+                )
+                nc.tensor.matmul_mx(
+                    out=o,
+                    lhsT=iq_t[b][:, i * P : (i + 1) * P].bitcast(FP8X4),
+                    lhsT_scale=isc_t[b][:, i * P : (i + 1) * P],
+                    rhs=wq[:, 256:512].bitcast(FP8X4),
+                    rhs_scale=wsc[:, 256:512],
+                    start=False,
+                    stop=True,
+                )
+            ob_t[b] = ob
+
+        def add_bias(b):
+            r = b // 2
+            if b % 2 == 0:
+                v_t[r] = vpool.tile([P, 1024], F32, name="v")
+            nc.vector.tensor_tensor(
+                out=v_t[r][:, (b % 2) * 512 : (b % 2 + 1) * 512],
+                in0=ob_t[b][:],
+                in1=bias2[:].rearrange("p i f -> p (i f)"),
+                op=ALU.add,
+            )
+
+        def silu_store(r):
+            nc.scalar.activation(out=v_t[r][:], in_=v_t[r][:], func=AF.Silu)
+            nc.sync.dma_start(out=ov[:, 4 * r : 4 * r + 4, :], in_=v_t[r][:].rearrange("p (i f) -> p i f", i=4))
+
+        def ok(b):
+            return 0 <= b < NB
+
+        def act_takes(b, k):
+            if b == 0:
+                return True
+            return k == 1
+
+        for b in range(4):
+            load(b)
+        next_load = 4
+        prep_pre1()
+
+        banks = [(m, jp) for m in range(3) for jp in range(2)]
+        for n in range(-2, NB + 2):
+            if ok(n):
+                for m, jp in banks[:4]:
+                    mm1(n, m, jp)
+            if ok(n - 2):
+                mm2(n - 2)
+            if ok(n):
+                for m, jp in banks[:2]:
+                    square(n, m, jp)
+                for m, jp in banks[4:]:
+                    mm1(n, m, jp)
+            if ok(n + 1):
+                for k in range(3):
+                    if not act_takes(n + 1, k):
+                        evac(n + 1, k, False)
+            if ok(n - 2):
+                add_bias(n - 2)
+            if ok(n):
+                for m, jp in banks[2:4]:
+                    square(n, m, jp)
+                add1(n)
+            if ok(n + 1):
+                for k in range(3):
+                    if act_takes(n + 1, k):
+                        evac(n + 1, k, True)
+                quant_block(n + 1)
+            if n == -1:
+                prep_w()
+            if ok(n):
+                for m, jp in banks[4:]:
+                    square(n, m, jp)
+                add2(n)
+            if ok(n + 2):
+                transposes_h(n + 2)
+                for m in range(3):
+                    transposes_x(n + 2, m)
+                if next_load < NB:
+                    load(next_load)
+                    next_load += 1
+                evac(n + 2, 3, True)
+            if ok(n - 1):
+                root(n - 1)
+                quant_inv(n - 1)
+        for r in range(NB // 2):
+            silu_store(r)

@@ -233,9 +233,9 @@ def tile_equivariantfeedforward_pa_t_kernel(tc, h, x1, pre1, w1_0, b1_0, out):
             return 0 <= b < NB
 
         def act_takes(b, k):
-            if b == 0:
+            if b < 2:
                 return True
-            return k == 1
+            return k == 1 or k == 3
 
         for b in range(4):
             load(b)
@@ -244,47 +244,48 @@ def tile_equivariantfeedforward_pa_t_kernel(tc, h, x1, pre1, w1_0, b1_0, out):
 
         banks = [(m, jp) for m in range(3) for jp in range(2)]
         for n in range(-2, NB + 2):
-            if ok(n):
-                for m, jp in banks[:4]:
-                    mm1(n, m, jp)
-            if ok(n - 2):
-                mm2(n - 2)
-            if ok(n):
-                for m, jp in banks[:2]:
-                    square(n, m, jp)
-                for m, jp in banks[4:]:
-                    mm1(n, m, jp)
-            if ok(n + 1):
-                for k in range(3):
-                    if not act_takes(n + 1, k):
-                        evac(n + 1, k, False)
-            if ok(n - 2):
-                add_bias(n - 2)
-            if ok(n):
-                for m, jp in banks[2:4]:
-                    square(n, m, jp)
-                add1(n)
-            if ok(n + 1):
-                for k in range(3):
-                    if act_takes(n + 1, k):
-                        evac(n + 1, k, True)
-                quant_block(n + 1)
-            if n == -1:
-                prep_w()
-            if ok(n):
-                for m, jp in banks[4:]:
-                    square(n, m, jp)
-                add2(n)
-            if ok(n + 2):
-                transposes_h(n + 2)
-                for m in range(3):
-                    transposes_x(n + 2, m)
-                if next_load < NB:
-                    load(next_load)
-                    next_load += 1
-                evac(n + 2, 3, True)
-            if ok(n - 1):
-                root(n - 1)
-                quant_inv(n - 1)
+            t = n + 2
+            for g in range(3):
+                pair = banks[2 * g : 2 * g + 2]
+                if ok(n):
+                    for m, jp in pair:
+                        mm1(n, m, jp)
+                if g == 1 and ok(n - 2):
+                    mm2(n - 2)
+                if ok(t):
+                    if g == 0:
+                        transposes_h(t)
+                    transposes_x(t, g)
+                if ok(n):
+                    for m, jp in pair:
+                        square(n, m, jp)
+                if g == 0:
+                    if ok(t - 1):
+                        evac(t - 1, 2, act_takes(t - 1, 2))
+                    if ok(t):
+                        evac(t, 3, act_takes(t, 3))
+                    if ok(n - 1):
+                        add2(n - 1)
+                    if ok(t - 1):
+                        quant_block(t - 1)
+                    if n == -1:
+                        prep_w()
+                if g == 1:
+                    if ok(t):
+                        evac(t, 0, act_takes(t, 0))
+                    if ok(n):
+                        add1(n)
+                    if ok(n - 1):
+                        root(n - 1)
+                if g == 2:
+                    if ok(t):
+                        evac(t, 1, act_takes(t, 1))
+                    if ok(n - 1):
+                        quant_inv(n - 1)
+                    if ok(n - 2):
+                        add_bias(n - 2)
+                    if ok(t) and next_load < NB:
+                        load(next_load)
+                        next_load += 1
         for r in range(NB // 2):
             silu_store(r)

@@ -29,18 +29,16 @@ def tile_equivariantfeedforward_pa_t_kernel(tc, h, x1, pre1, w1_0, b1_0, out):
         const = ctx.enter_context(tc.tile_pool(name="const", bufs=1))
         xpool = ctx.enter_context(tc.tile_pool(name="xpool", bufs=4))
         gpool = ctx.enter_context(tc.tile_pool(name="gpool", bufs=2))
-        cpool = ctx.enter_context(tc.tile_pool(name="cpool", bufs=5))
+        cpool = ctx.enter_context(tc.tile_pool(name="cpool", bufs=3))
         spool = ctx.enter_context(tc.tile_pool(name="spool", bufs=6))
         apool = ctx.enter_context(tc.tile_pool(name="apool", bufs=2))
-        ipool = ctx.enter_context(tc.tile_pool(name="ipool", bufs=3))
         vpool = ctx.enter_context(tc.tile_pool(name="vpool", bufs=8))
         ps_tp = ctx.enter_context(tc.psum_pool(name="ps_tp", bufs=3))
-        ps_pm = ctx.enter_context(tc.psum_pool(name="ps_pm", bufs=4))
-        ps_ob = ctx.enter_context(tc.psum_pool(name="ps_ob", bufs=1))
+        ps_pm = ctx.enter_context(tc.psum_pool(name="ps_pm", bufs=5))
         ctx.enter_context(tc.manual_schedule())
 
         xs_t, hs_t, tp_t, xg_t, cod_t, scl_t = {}, {}, {}, {}, {}, {}
-        pm_t, s_t, t_t, a_t, ig_t, iq_t, isc_t, ob_t, v_t = {}, {}, {}, {}, {}, {}, {}, {}, {}
+        pm_t, s_t, t_t, a_t, ig_t, v_t = {}, {}, {}, {}, {}, {}
 
         ident_bf = const.tile([P, P], BF16, name="ident_bf")
         ident_f = const.tile([P, P], F32, name="ident_f")
@@ -75,6 +73,10 @@ def tile_equivariantfeedforward_pa_t_kernel(tc, h, x1, pre1, w1_0, b1_0, out):
         wq = const.tile([P, 512], U32, name="wq", align_bytes=64)
         wsc = const.tile([P, 512], U8, name="wsc", align_bytes=64)
         bias2 = const.tile([P, 2, 256], F32, name="bias2")
+        hq = const.tile([P, NB * BT], U32, name="hq", align_bytes=64)
+        hsc = const.tile([P, NB * BT], U8, name="hsc", align_bytes=64)
+        iq = const.tile([P, NB * BT], U32, name="iq", align_bytes=64)
+        isc = const.tile([P, NB * BT], U8, name="isc", align_bytes=64)
 
         def prep_pre1():
             nc.vector.tensor_copy(
@@ -93,13 +95,13 @@ def tile_equivariantfeedforward_pa_t_kernel(tc, h, x1, pre1, w1_0, b1_0, out):
                 nc.vector.tensor_copy(out=bias2[:, i, :], in_=bb16[:])
 
         def load(b):
-            hs = xpool.tile([P, 2, 512], BF16, name="hs")
-            nc.sync.dma_start(out=hs[:], in_=hv[:, 2 * b : 2 * b + 2, :])
             xs = xpool.tile([P, 4, 768], BF16, name="xs")
             pieces = 2 if b == 0 else 1
             step = 4 // pieces
             for g in range(0, 4, step):
                 nc.sync.dma_start(out=xs[:, g : g + step, :], in_=xv[:, 4 * b + g : 4 * b + g + step, :])
+            hs = xpool.tile([P, 2, 512], BF16, name="hs")
+            nc.sync.dma_start(out=hs[:], in_=hv[:, 2 * b : 2 * b + 2, :])
             xs_t[b] = xs
             hs_t[b] = hs
 
@@ -136,12 +138,17 @@ def tile_equivariantfeedforward_pa_t_kernel(tc, h, x1, pre1, w1_0, b1_0, out):
             else:
                 nc.vector.tensor_copy(out=dst, in_=src)
 
-        def quant_block(b):
-            cod = cpool.tile([P, 1024], U32, name="cod", align_bytes=64)
-            scl = cpool.tile([P, 1024], U8, name="scl", align_bytes=64)
-            nc.vector.quantize_mx(out=cod[:].bitcast(FP8X4), scales=scl[:], in_=xg_t[b][:])
-            cod_t[b] = cod
-            scl_t[b] = scl
+        def quant(b, k):
+            grouped = xg_t[b][:, k * 1024 : (k + 1) * 1024]
+            if k == 3:
+                cols = slice(b * BT, (b + 1) * BT)
+                nc.vector.quantize_mx(out=hq[:, cols].bitcast(FP8X4), scales=hsc[:, cols], in_=grouped)
+                return
+            if b not in cod_t:
+                cod_t[b] = cpool.tile([P, 768], U32, name="cod", align_bytes=64)
+                scl_t[b] = cpool.tile([P, 768], U8, name="scl", align_bytes=64)
+            cols = slice(k * BT, (k + 1) * BT)
+            nc.vector.quantize_mx(out=cod_t[b][:, cols].bitcast(FP8X4), scales=scl_t[b][:, cols], in_=grouped)
 
         def mm1(b, m, jp):
             pm = ps_pm.tile([P, 512], F32, name="pm")
@@ -185,19 +192,18 @@ def tile_equivariantfeedforward_pa_t_kernel(tc, h, x1, pre1, w1_0, b1_0, out):
             )
 
         def quant_inv(b):
-            iq_t[b] = ipool.tile([P, 256], U32, name="iq", align_bytes=64)
-            isc_t[b] = ipool.tile([P, 256], U8, name="isc", align_bytes=64)
-            nc.vector.quantize_mx(out=iq_t[b][:].bitcast(FP8X4), scales=isc_t[b][:], in_=ig_t[b][:])
+            cols = slice(b * BT, (b + 1) * BT)
+            nc.vector.quantize_mx(out=iq[:, cols].bitcast(FP8X4), scales=isc[:, cols], in_=ig_t[b][:])
 
-        def mm2(b):
-            ob = ps_ob.tile([P, 512], F32, name="ob")
+        def mm2_bias(b):
+            ob = ps_pm.tile([P, 512], F32, name="pm")
             for i in range(2):
                 o = ob[:, i * 256 : (i + 1) * 256]
-                c0 = 768 + i * P
+                cols = slice(b * BT + i * P, b * BT + (i + 1) * P)
                 nc.tensor.matmul_mx(
                     out=o,
-                    lhsT=cod_t[b][:, c0 : c0 + P].bitcast(FP8X4),
-                    lhsT_scale=scl_t[b][:, c0 : c0 + P],
+                    lhsT=hq[:, cols].bitcast(FP8X4),
+                    lhsT_scale=hsc[:, cols],
                     rhs=wq[:, 0:256].bitcast(FP8X4),
                     rhs_scale=wsc[:, 0:256],
                     start=True,
@@ -205,22 +211,19 @@ def tile_equivariantfeedforward_pa_t_kernel(tc, h, x1, pre1, w1_0, b1_0, out):
                 )
                 nc.tensor.matmul_mx(
                     out=o,
-                    lhsT=iq_t[b][:, i * P : (i + 1) * P].bitcast(FP8X4),
-                    lhsT_scale=isc_t[b][:, i * P : (i + 1) * P],
+                    lhsT=iq[:, cols].bitcast(FP8X4),
+                    lhsT_scale=isc[:, cols],
                     rhs=wq[:, 256:512].bitcast(FP8X4),
                     rhs_scale=wsc[:, 256:512],
                     start=False,
                     stop=True,
                 )
-            ob_t[b] = ob
-
-        def add_bias(b):
             r = b // 2
             if b % 2 == 0:
                 v_t[r] = vpool.tile([P, 1024], F32, name="v")
             nc.vector.tensor_tensor(
                 out=v_t[r][:, (b % 2) * 512 : (b % 2 + 1) * 512],
-                in0=ob_t[b][:],
+                in0=ob[:],
                 in1=bias2[:].rearrange("p i f -> p (i f)"),
                 op=ALU.add,
             )
@@ -233,59 +236,67 @@ def tile_equivariantfeedforward_pa_t_kernel(tc, h, x1, pre1, w1_0, b1_0, out):
             return 0 <= b < NB
 
         def act_takes(b, k):
-            if b < 2:
+            if b < 1:
                 return True
-            return k == 1 or k == 3
+            return k == 3 or (k == 1 and b % 2 == 0)
 
         for b in range(4):
             load(b)
         next_load = 4
         prep_pre1()
 
-        banks = [(m, jp) for m in range(3) for jp in range(2)]
-        for n in range(-2, NB + 2):
-            t = n + 2
+        next_mm2 = 0
+        for n in range(-1, NB + 1):
+            t = n + 1
             for g in range(3):
-                pair = banks[2 * g : 2 * g + 2]
                 if ok(n):
-                    for m, jp in pair:
-                        mm1(n, m, jp)
-                if g == 1 and ok(n - 2):
-                    mm2(n - 2)
+                    for jp in range(2):
+                        mm1(n, g, jp)
                 if ok(t):
+                    transposes_x(t, g)
                     if g == 0:
                         transposes_h(t)
-                    transposes_x(t, g)
                 if ok(n):
-                    for m, jp in pair:
-                        square(n, m, jp)
+                    for jp in range(2):
+                        square(n, g, jp)
                 if g == 0:
-                    if ok(t - 1):
-                        evac(t - 1, 2, act_takes(t - 1, 2))
+                    if ok(n):
+                        evac(n, 2, act_takes(n, 2))
                     if ok(t):
                         evac(t, 3, act_takes(t, 3))
                     if ok(n - 1):
                         add2(n - 1)
-                    if ok(t - 1):
-                        quant_block(t - 1)
-                    if n == -1:
-                        prep_w()
+                    if ok(n):
+                        quant(n, 2)
                 if g == 1:
                     if ok(t):
                         evac(t, 0, act_takes(t, 0))
-                    if ok(n):
-                        add1(n)
                     if ok(n - 1):
                         root(n - 1)
+                    if ok(t):
+                        quant(t, 3)
+                        quant(t, 0)
                 if g == 2:
                     if ok(t):
                         evac(t, 1, act_takes(t, 1))
+                    if ok(n):
+                        add1(n)
                     if ok(n - 1):
                         quant_inv(n - 1)
-                    if ok(n - 2):
-                        add_bias(n - 2)
+                    if ok(t):
+                        quant(t, 1)
                     if ok(t) and next_load < NB:
                         load(next_load)
                         next_load += 1
+                    if n == NB - 1:
+                        prep_w()
+            if n >= NB - 1:
+                for rep in range(2):
+                    if next_mm2 <= n - 1:
+                        mm2_bias(next_mm2)
+                        next_mm2 += 1
         for r in range(NB // 2):
+            while next_mm2 < min(NB, 2 * r + 4):
+                mm2_bias(next_mm2)
+                next_mm2 += 1
             silu_store(r)

@@ -218,19 +218,17 @@ def tile_equivariantfeedforward_pa_t_kernel(tc, h, x1, pre1, w1_0, b1_0, out):
                     start=False,
                     stop=True,
                 )
-            r = b // 2
-            if b % 2 == 0:
-                v_t[r] = vpool.tile([P, 1024], F32, name="v")
+            v_t[b] = vpool.tile([P, 512], F32, name="v")
             nc.vector.tensor_tensor(
-                out=v_t[r][:, (b % 2) * 512 : (b % 2 + 1) * 512],
+                out=v_t[b][:],
                 in0=ob[:],
                 in1=bias2[:].rearrange("p i f -> p (i f)"),
                 op=ALU.add,
             )
 
-        def silu_store(r):
-            nc.scalar.activation(out=v_t[r][:], in_=v_t[r][:], func=AF.Silu)
-            nc.sync.dma_start(out=ov[:, 4 * r : 4 * r + 4, :], in_=v_t[r][:].rearrange("p (i f) -> p i f", i=4))
+        def silu_store(b):
+            nc.scalar.activation(out=v_t[b][:], in_=v_t[b][:], func=AF.Silu)
+            nc.sync.dma_start(out=ov[:, 2 * b : 2 * b + 2, :], in_=v_t[b][:].rearrange("p (i f) -> p i f", i=2))
 
         def ok(b):
             return 0 <= b < NB
@@ -246,7 +244,7 @@ def tile_equivariantfeedforward_pa_t_kernel(tc, h, x1, pre1, w1_0, b1_0, out):
         prep_pre1()
 
         next_mm2 = 0
-        for n in range(-1, NB + 1):
+        for n in range(-1, NB + 2):
             t = n + 1
             for g in range(3):
                 if ok(n):
@@ -268,35 +266,33 @@ def tile_equivariantfeedforward_pa_t_kernel(tc, h, x1, pre1, w1_0, b1_0, out):
                         add2(n - 1)
                     if ok(n):
                         quant(n, 2)
+                    if ok(n - 2):
+                        quant_inv(n - 2)
                 if g == 1:
                     if ok(t):
                         evac(t, 0, act_takes(t, 0))
-                    if ok(n - 1):
-                        root(n - 1)
                     if ok(t):
                         quant(t, 3)
                         quant(t, 0)
                 if g == 2:
                     if ok(t):
                         evac(t, 1, act_takes(t, 1))
+                    if ok(n - 1):
+                        root(n - 1)
                     if ok(n):
                         add1(n)
-                    if ok(n - 1):
-                        quant_inv(n - 1)
                     if ok(t):
                         quant(t, 1)
                     if ok(t) and next_load < NB:
                         load(next_load)
                         next_load += 1
-                    if n == NB - 1:
+                    if n == -1:
                         prep_w()
-            if n >= NB - 1:
-                for rep in range(2):
-                    if next_mm2 <= n - 1:
-                        mm2_bias(next_mm2)
-                        next_mm2 += 1
-        for r in range(NB // 2):
-            while next_mm2 < min(NB, 2 * r + 4):
+                if n >= NB - 1 and (n, g) != (NB - 1, 0):
+                    mm2_bias(next_mm2)
+                    next_mm2 += 1
+        for b in range(NB):
+            while next_mm2 < min(NB, b + 4):
                 mm2_bias(next_mm2)
                 next_mm2 += 1
-            silu_store(r)
+            silu_store(b)

@@ -79,10 +79,10 @@ def tile_equivariantfeedforward_pa_t_kernel(tc, h, x1, pre1, w1_0, b1_0, out):
         isc = const.tile([P, NB * BT], U8, name="isc", align_bytes=64)
 
         def prep_pre1():
-            nc.vector.tensor_copy(
-                out=pg[:].rearrange("p (j q t) -> p j q t", j=4, t=4),
-                in_=pw[:].rearrange("p t (q j) -> p j q t", j=4),
-            )
+            pg_v = pg[:].rearrange("p (j q t) -> p j q t", j=4, t=4)
+            pw_v = pw[:].rearrange("p t (q j) -> p j q t", j=4)
+            nc.vector.tensor_copy(out=pg_v[:, 0:2], in_=pw_v[:, 0:2])
+            nc.scalar.copy(out=pg_v[:, 2:4], in_=pw_v[:, 2:4])
             nc.vector.quantize_mx(out=pq[:].bitcast(FP8X4), scales=psc[:], in_=pg[:])
 
         def prep_w():
@@ -96,7 +96,7 @@ def tile_equivariantfeedforward_pa_t_kernel(tc, h, x1, pre1, w1_0, b1_0, out):
 
         def load(b):
             xs = xpool.tile([P, 4, 768], BF16, name="xs")
-            pieces = 2 if b == 0 else 1
+            pieces = 4 if b == 0 else 1
             step = 4 // pieces
             for g in range(0, 4, step):
                 nc.sync.dma_start(out=xs[:, g : g + step, :], in_=xv[:, 4 * b + g : 4 * b + g + step, :])
@@ -122,6 +122,16 @@ def tile_equivariantfeedforward_pa_t_kernel(tc, h, x1, pre1, w1_0, b1_0, out):
                     c = 2 * g + u
                     nc.tensor.transpose(tp[:, c * P : (c + 1) * P], xg4[:, u, :, m], ident_bf[:])
             tp_t[(b, m)] = tp
+
+        def transposes_x_first():
+            for m in range(3):
+                tp_t[(0, m)] = ps_tp.tile([P, 1024], BF16, name="tp")
+            for g in range(4):
+                xg4 = xs_t[0][:, g, :].rearrange("p (u d m) -> p u d m", u=2, m=3)
+                for m in range(3):
+                    for u in range(2):
+                        c = 2 * g + u
+                        nc.tensor.transpose(tp_t[(0, m)][:, c * P : (c + 1) * P], xg4[:, u, :, m], ident_bf[:])
 
         def evac(b, k, on_act):
             if b not in xg_t:
@@ -236,15 +246,23 @@ def tile_equivariantfeedforward_pa_t_kernel(tc, h, x1, pre1, w1_0, b1_0, out):
         def act_takes(b, k):
             if b < 1:
                 return True
-            return k == 3 or (k == 1 and b % 2 == 0)
+            return k == 3
 
         for b in range(4):
             load(b)
         next_load = 4
         prep_pre1()
 
+        transposes_x_first()
+        evac(0, 0, True)
+        evac(0, 1, False)
+        evac(0, 2, True)
+        for k in range(3):
+            quant(0, k)
+        prep_w()
+
         next_mm2 = 0
-        for n in range(-1, NB + 2):
+        for n in range(0, NB + 2):
             t = n + 1
             for g in range(3):
                 if ok(n):
@@ -254,18 +272,24 @@ def tile_equivariantfeedforward_pa_t_kernel(tc, h, x1, pre1, w1_0, b1_0, out):
                     transposes_x(t, g)
                     if g == 0:
                         transposes_h(t)
+                if n == 0 and g == 0:
+                    transposes_h(0)
                 if ok(n):
                     for jp in range(2):
                         square(n, g, jp)
                 if g == 0:
-                    if ok(n):
+                    if 1 <= n < NB:
                         evac(n, 2, act_takes(n, 2))
                     if ok(t):
                         evac(t, 3, act_takes(t, 3))
+                    if n == 0:
+                        evac(0, 3, True)
                     if ok(n - 1):
                         add2(n - 1)
-                    if ok(n):
+                    if 1 <= n < NB:
                         quant(n, 2)
+                    if n == 0:
+                        quant(0, 3)
                     if ok(n - 2):
                         quant_inv(n - 2)
                 if g == 1:
@@ -286,8 +310,6 @@ def tile_equivariantfeedforward_pa_t_kernel(tc, h, x1, pre1, w1_0, b1_0, out):
                     if ok(t) and next_load < NB:
                         load(next_load)
                         next_load += 1
-                    if n == -1:
-                        prep_w()
                 if n >= NB - 1 and (n, g) != (NB - 1, 0):
                     mm2_bias(next_mm2)
                     next_mm2 += 1

@@ -178,7 +178,11 @@ def tile_equivariantfeedforward_pa_t_kernel(tc, h, x1, pre1, w1_0, b1_0, out):
         def square(b, m, jp):
             if jp == 0:
                 s_t[(b, m)] = spool.tile([P, 1024], F32, name="sq")
-            nc.scalar.activation(out=s_t[(b, m)][:, jp * 512 : (jp + 1) * 512], in_=pm_t[(b, m, jp)][:], func=AF.Square)
+            nc.scalar.activation(
+                out=s_t[(b, m)][:, jp * 512 : (jp + 1) * 512].rearrange("p (t j) -> p t j", j=2),
+                in_=pm_t[(b, m, jp)][:].rearrange("p (j t) -> p t j", j=2),
+                func=AF.Square,
+            )
 
         def add1(b):
             t_t[b] = apool.tile([P, 1024], F32, name="t01")
@@ -186,12 +190,7 @@ def tile_equivariantfeedforward_pa_t_kernel(tc, h, x1, pre1, w1_0, b1_0, out):
 
         def add2(b):
             a_t[b] = apool.tile([P, 1024], F32, name="a012")
-            nc.vector.tensor_tensor(
-                out=a_t[b][:].rearrange("p (c t j) -> p c t j", c=2, j=2),
-                in0=t_t[b][:].rearrange("p (c j t) -> p c t j", c=2, j=2),
-                in1=s_t[(b, 2)][:].rearrange("p (c j t) -> p c t j", c=2, j=2),
-                op=ALU.add,
-            )
+            nc.vector.tensor_tensor(out=a_t[b][:], in0=t_t[b][:], in1=s_t[(b, 2)][:], op=ALU.add)
 
         def root(b):
             ig_t[b] = apool.tile([P, 1024], BF16, name="ig", align_bytes=64)
@@ -246,7 +245,7 @@ def tile_equivariantfeedforward_pa_t_kernel(tc, h, x1, pre1, w1_0, b1_0, out):
         def act_takes(b, k):
             if b < 1:
                 return True
-            return k == 3
+            return k == 3 or (k == 1 and b % 2 == 0)
 
         for b in range(4):
             load(b)

@@ -38,7 +38,7 @@ def tile_equivariantfeedforward_pa_t_kernel(tc, h, x1, pre1, w1_0, b1_0, out):
         ctx.enter_context(tc.manual_schedule())
 
         xs_t, hs_t, tp_t, xg_t, cod_t, scl_t = {}, {}, {}, {}, {}, {}
-        pm_t, s_t, t_t, a_t, ig_t, v_t = {}, {}, {}, {}, {}, {}
+        pm_t, s_t, t_t, a_t, ig_t, v_t, xm_t = {}, {}, {}, {}, {}, {}, {}
 
         ident_bf = const.tile([P, P], BF16, name="ident_bf")
         ident_f = const.tile([P, P], F32, name="ident_f")
@@ -53,6 +53,11 @@ def tile_equivariantfeedforward_pa_t_kernel(tc, h, x1, pre1, w1_0, b1_0, out):
         pre_v = pre1.rearrange("(j u p) e -> u p j e", j=2, u=2)
         for u in range(2):
             nc.scalar.dma_start(out=pw[:, 2 * u : 2 * u + 2, :], in_=pre_v[u])
+        pw2 = const.tile([P, 4, 512], BF16, name="pw2")
+        nc.scalar.dma_start(
+            out=pw2[:].rearrange("p (j e) c -> p j (e c)", j=2),
+            in_=pre1.rearrange("(j p e) c -> p j (e c)", j=2, e=2),
+        )
         wr = const.tile([P, 2, 4, 256], BF16, name="wr")
         nc.scalar.dma_start(
             out=wr[:, 0].rearrange("p (u e) f -> p u (e f)", u=2),
@@ -79,11 +84,22 @@ def tile_equivariantfeedforward_pa_t_kernel(tc, h, x1, pre1, w1_0, b1_0, out):
         isc = const.tile([P, NB * BT], U8, name="isc", align_bytes=64)
 
         def prep_pre1():
-            pg_v = pg[:].rearrange("p (j q t) -> p j q t", j=4, t=4)
-            pw_v = pw[:].rearrange("p t (q j) -> p j q t", j=4)
-            nc.vector.tensor_copy(out=pg_v[:, 0:2], in_=pw_v[:, 0:2])
-            nc.scalar.copy(out=pg_v[:, 2:4], in_=pw_v[:, 2:4])
+            nc.vector.tensor_copy(
+                out=pg[:].rearrange("p (j q t) -> p j q t", j=4, t=4),
+                in_=pw[:].rearrange("p t (q j) -> p j q t", j=4),
+            )
             nc.vector.quantize_mx(out=pq[:].bitcast(FP8X4), scales=psc[:], in_=pg[:])
+
+        pg2 = const.tile([P, 2048], BF16, name="pg2", align_bytes=64)
+        pq2 = const.tile([P, 512], U32, name="pq2", align_bytes=64)
+        psc2 = const.tile([P, 512], U8, name="psc2", align_bytes=64)
+
+        def prep_pre1_second():
+            nc.vector.tensor_copy(
+                out=pg2[:].rearrange("p (j q t) -> p j q t", j=4, t=4),
+                in_=pw2[:].rearrange("p t (q j) -> p j q t", j=4),
+            )
+            nc.vector.quantize_mx(out=pq2[:].bitcast(FP8X4), scales=psc2[:], in_=pg2[:])
 
         def prep_w():
             nc.vector.tensor_copy(
@@ -96,7 +112,7 @@ def tile_equivariantfeedforward_pa_t_kernel(tc, h, x1, pre1, w1_0, b1_0, out):
 
         def load(b):
             xs = xpool.tile([P, 4, 768], BF16, name="xs")
-            pieces = 4 if b == 0 else 1
+            pieces = 2 if b == 0 else 1
             step = 4 // pieces
             for g in range(0, 4, step):
                 nc.sync.dma_start(out=xs[:, g : g + step, :], in_=xv[:, 4 * b + g : 4 * b + g + step, :])
@@ -114,7 +130,19 @@ def tile_equivariantfeedforward_pa_t_kernel(tc, h, x1, pre1, w1_0, b1_0, out):
                     nc.tensor.transpose(th[:, c * P : (c + 1) * P], hw[:, i, u * P : (u + 1) * P], ident_f[:])
             tp_t[(b, 3)] = th
 
+        def sort_out_last_component(b):
+            xm = xpool.tile([P, 4, 256], BF16, name="xm")
+            nc.vector.tensor_copy(out=xm[:], in_=xs_t[b][:].rearrange("p g (d m) -> p g d m", m=3)[:, :, :, 2])
+            xm_t[b] = xm
+
         def transposes_x(b, m):
+            if m == 2:
+                tw = ps_tp.tile([P, 512], F32, name="tp")
+                xw = xm_t[b][:].bitcast(F32)
+                for g in range(4):
+                    nc.tensor.transpose(tw[:, g * P : (g + 1) * P], xw[:, g, :], ident_f[:])
+                tp_t[(b, m)] = tw
+                return
             tp = ps_tp.tile([P, 1024], BF16, name="tp")
             for g in range(4):
                 xg4 = xs_t[b][:, g, :].rearrange("p (u d m) -> p u d m", u=2, m=3)
@@ -123,21 +151,13 @@ def tile_equivariantfeedforward_pa_t_kernel(tc, h, x1, pre1, w1_0, b1_0, out):
                     nc.tensor.transpose(tp[:, c * P : (c + 1) * P], xg4[:, u, :, m], ident_bf[:])
             tp_t[(b, m)] = tp
 
-        def transposes_x_first():
-            for m in range(3):
-                tp_t[(0, m)] = ps_tp.tile([P, 1024], BF16, name="tp")
-            for g in range(4):
-                xg4 = xs_t[0][:, g, :].rearrange("p (u d m) -> p u d m", u=2, m=3)
-                for m in range(3):
-                    for u in range(2):
-                        c = 2 * g + u
-                        nc.tensor.transpose(tp_t[(0, m)][:, c * P : (c + 1) * P], xg4[:, u, :, m], ident_bf[:])
-
         def evac(b, k, on_act):
             if b not in xg_t:
                 xg_t[b] = gpool.tile([P, 4096], BF16, name="xg", align_bytes=64)
             dst = xg_t[b][:, k * 1024 : (k + 1) * 1024].bitcast(F32)
-            if k < 3:
+            if k == 2:
+                src = tp_t[(b, k)][:]
+            elif k < 2:
                 src = tp_t[(b, k)][:].bitcast(F32).rearrange("p (g u a) -> p g a u", g=4, u=2)
                 dst = dst.rearrange("p (g a u) -> p g a u", g=4, u=2)
             else:
@@ -162,12 +182,13 @@ def tile_equivariantfeedforward_pa_t_kernel(tc, h, x1, pre1, w1_0, b1_0, out):
 
         def mm1(b, m, jp):
             pm = ps_pm.tile([P, 512], F32, name="pm")
+            wq1, ws1 = (pq2, psc2) if m == 2 else (pq, psc)
             for j2 in range(2):
                 j = 2 * jp + j2
                 nc.tensor.matmul_mx(
                     out=pm[:, j2 * BT : (j2 + 1) * BT],
-                    lhsT=pq[:, j * P : (j + 1) * P].bitcast(FP8X4),
-                    lhsT_scale=psc[:, j * P : (j + 1) * P],
+                    lhsT=wq1[:, j * P : (j + 1) * P].bitcast(FP8X4),
+                    lhsT_scale=ws1[:, j * P : (j + 1) * P],
                     rhs=cod_t[b][:, m * BT : (m + 1) * BT].bitcast(FP8X4),
                     rhs_scale=scl_t[b][:, m * BT : (m + 1) * BT],
                     start=True,
@@ -178,11 +199,7 @@ def tile_equivariantfeedforward_pa_t_kernel(tc, h, x1, pre1, w1_0, b1_0, out):
         def square(b, m, jp):
             if jp == 0:
                 s_t[(b, m)] = spool.tile([P, 1024], F32, name="sq")
-            nc.scalar.activation(
-                out=s_t[(b, m)][:, jp * 512 : (jp + 1) * 512].rearrange("p (t j) -> p t j", j=2),
-                in_=pm_t[(b, m, jp)][:].rearrange("p (j t) -> p t j", j=2),
-                func=AF.Square,
-            )
+            nc.scalar.activation(out=s_t[(b, m)][:, jp * 512 : (jp + 1) * 512], in_=pm_t[(b, m, jp)][:], func=AF.Square)
 
         def add1(b):
             t_t[b] = apool.tile([P, 1024], F32, name="t01")
@@ -190,7 +207,12 @@ def tile_equivariantfeedforward_pa_t_kernel(tc, h, x1, pre1, w1_0, b1_0, out):
 
         def add2(b):
             a_t[b] = apool.tile([P, 1024], F32, name="a012")
-            nc.vector.tensor_tensor(out=a_t[b][:], in0=t_t[b][:], in1=s_t[(b, 2)][:], op=ALU.add)
+            nc.vector.tensor_tensor(
+                out=a_t[b][:].rearrange("p (c t j) -> p c t j", c=2, j=2),
+                in0=t_t[b][:].rearrange("p (c j t) -> p c t j", c=2, j=2),
+                in1=s_t[(b, 2)][:].rearrange("p (c j t) -> p c t j", c=2, j=2),
+                op=ALU.add,
+            )
 
         def root(b):
             ig_t[b] = apool.tile([P, 1024], BF16, name="ig", align_bytes=64)
@@ -245,23 +267,15 @@ def tile_equivariantfeedforward_pa_t_kernel(tc, h, x1, pre1, w1_0, b1_0, out):
         def act_takes(b, k):
             if b < 1:
                 return True
-            return k == 3 or (k == 1 and b % 2 == 0)
+            return k == 3 or k == 1
 
         for b in range(4):
             load(b)
         next_load = 4
         prep_pre1()
 
-        transposes_x_first()
-        evac(0, 0, True)
-        evac(0, 1, False)
-        evac(0, 2, True)
-        for k in range(3):
-            quant(0, k)
-        prep_w()
-
         next_mm2 = 0
-        for n in range(0, NB + 2):
+        for n in range(-1, NB + 2):
             t = n + 1
             for g in range(3):
                 if ok(n):
@@ -271,27 +285,25 @@ def tile_equivariantfeedforward_pa_t_kernel(tc, h, x1, pre1, w1_0, b1_0, out):
                     transposes_x(t, g)
                     if g == 0:
                         transposes_h(t)
-                if n == 0 and g == 0:
-                    transposes_h(0)
                 if ok(n):
                     for jp in range(2):
                         square(n, g, jp)
                 if g == 0:
-                    if 1 <= n < NB:
+                    if ok(n):
                         evac(n, 2, act_takes(n, 2))
                     if ok(t):
                         evac(t, 3, act_takes(t, 3))
-                    if n == 0:
-                        evac(0, 3, True)
                     if ok(n - 1):
                         add2(n - 1)
-                    if 1 <= n < NB:
+                    if ok(n):
                         quant(n, 2)
-                    if n == 0:
-                        quant(0, 3)
                     if ok(n - 2):
                         quant_inv(n - 2)
+                    if ok(t):
+                        sort_out_last_component(t)
                 if g == 1:
+                    if n == NB - 1:
+                        prep_w()
                     if ok(t):
                         evac(t, 0, act_takes(t, 0))
                     if ok(t):
@@ -309,6 +321,8 @@ def tile_equivariantfeedforward_pa_t_kernel(tc, h, x1, pre1, w1_0, b1_0, out):
                     if ok(t) and next_load < NB:
                         load(next_load)
                         next_load += 1
+                    if n == -1:
+                        prep_pre1_second()
                 if n >= NB - 1 and (n, g) != (NB - 1, 0):
                     mm2_bias(next_mm2)
                     next_mm2 += 1

@@ -38,7 +38,7 @@ def tile_equivariantfeedforward_pa_t_kernel(tc, h, x1, pre1, w1_0, b1_0, out):
         ctx.enter_context(tc.manual_schedule())
 
         xs_t, hs_t, tp_t, xg_t, cod_t, scl_t = {}, {}, {}, {}, {}, {}
-        pm_t, s_t, t_t, a_t, ig_t, v_t, xm_t = {}, {}, {}, {}, {}, {}, {}
+        pm_t, s_t, t_t, a_t, ig_t, v_t = {}, {}, {}, {}, {}, {}
 
         ident_bf = const.tile([P, P], BF16, name="ident_bf")
         ident_f = const.tile([P, P], F32, name="ident_f")
@@ -53,11 +53,6 @@ def tile_equivariantfeedforward_pa_t_kernel(tc, h, x1, pre1, w1_0, b1_0, out):
         pre_v = pre1.rearrange("(j u p) e -> u p j e", j=2, u=2)
         for u in range(2):
             nc.scalar.dma_start(out=pw[:, 2 * u : 2 * u + 2, :], in_=pre_v[u])
-        pw2 = const.tile([P, 4, 512], BF16, name="pw2")
-        nc.scalar.dma_start(
-            out=pw2[:].rearrange("p (j e) c -> p j (e c)", j=2),
-            in_=pre1.rearrange("(j p e) c -> p j (e c)", j=2, e=2),
-        )
         wr = const.tile([P, 2, 4, 256], BF16, name="wr")
         nc.scalar.dma_start(
             out=wr[:, 0].rearrange("p (u e) f -> p u (e f)", u=2),
@@ -90,17 +85,6 @@ def tile_equivariantfeedforward_pa_t_kernel(tc, h, x1, pre1, w1_0, b1_0, out):
             )
             nc.vector.quantize_mx(out=pq[:].bitcast(FP8X4), scales=psc[:], in_=pg[:])
 
-        pg2 = const.tile([P, 2048], BF16, name="pg2", align_bytes=64)
-        pq2 = const.tile([P, 512], U32, name="pq2", align_bytes=64)
-        psc2 = const.tile([P, 512], U8, name="psc2", align_bytes=64)
-
-        def prep_pre1_second():
-            nc.vector.tensor_copy(
-                out=pg2[:].rearrange("p (j q t) -> p j q t", j=4, t=4),
-                in_=pw2[:].rearrange("p t (q j) -> p j q t", j=4),
-            )
-            nc.vector.quantize_mx(out=pq2[:].bitcast(FP8X4), scales=psc2[:], in_=pg2[:])
-
         def prep_w():
             nc.vector.tensor_copy(
                 out=wg[:].rearrange("p (s f t) -> p s f t", s=2, t=4),
@@ -130,19 +114,7 @@ def tile_equivariantfeedforward_pa_t_kernel(tc, h, x1, pre1, w1_0, b1_0, out):
                     nc.tensor.transpose(th[:, c * P : (c + 1) * P], hw[:, i, u * P : (u + 1) * P], ident_f[:])
             tp_t[(b, 3)] = th
 
-        def sort_out_last_component(b):
-            xm = xpool.tile([P, 4, 256], BF16, name="xm")
-            nc.vector.tensor_copy(out=xm[:], in_=xs_t[b][:].rearrange("p g (d m) -> p g d m", m=3)[:, :, :, 2])
-            xm_t[b] = xm
-
         def transposes_x(b, m):
-            if m == 2:
-                tw = ps_tp.tile([P, 512], F32, name="tp")
-                xw = xm_t[b][:].bitcast(F32)
-                for g in range(4):
-                    nc.tensor.transpose(tw[:, g * P : (g + 1) * P], xw[:, g, :], ident_f[:])
-                tp_t[(b, m)] = tw
-                return
             tp = ps_tp.tile([P, 1024], BF16, name="tp")
             for g in range(4):
                 xg4 = xs_t[b][:, g, :].rearrange("p (u d m) -> p u d m", u=2, m=3)
@@ -155,9 +127,7 @@ def tile_equivariantfeedforward_pa_t_kernel(tc, h, x1, pre1, w1_0, b1_0, out):
             if b not in xg_t:
                 xg_t[b] = gpool.tile([P, 4096], BF16, name="xg", align_bytes=64)
             dst = xg_t[b][:, k * 1024 : (k + 1) * 1024].bitcast(F32)
-            if k == 2:
-                src = tp_t[(b, k)][:]
-            elif k < 2:
+            if k < 3:
                 src = tp_t[(b, k)][:].bitcast(F32).rearrange("p (g u a) -> p g a u", g=4, u=2)
                 dst = dst.rearrange("p (g a u) -> p g a u", g=4, u=2)
             else:
@@ -182,13 +152,12 @@ def tile_equivariantfeedforward_pa_t_kernel(tc, h, x1, pre1, w1_0, b1_0, out):
 
         def mm1(b, m, jp):
             pm = ps_pm.tile([P, 512], F32, name="pm")
-            wq1, ws1 = (pq2, psc2) if m == 2 else (pq, psc)
             for j2 in range(2):
                 j = 2 * jp + j2
                 nc.tensor.matmul_mx(
                     out=pm[:, j2 * BT : (j2 + 1) * BT],
-                    lhsT=wq1[:, j * P : (j + 1) * P].bitcast(FP8X4),
-                    lhsT_scale=ws1[:, j * P : (j + 1) * P],
+                    lhsT=pq[:, j * P : (j + 1) * P].bitcast(FP8X4),
+                    lhsT_scale=psc[:, j * P : (j + 1) * P],
                     rhs=cod_t[b][:, m * BT : (m + 1) * BT].bitcast(FP8X4),
                     rhs_scale=scl_t[b][:, m * BT : (m + 1) * BT],
                     start=True,
@@ -203,7 +172,9 @@ def tile_equivariantfeedforward_pa_t_kernel(tc, h, x1, pre1, w1_0, b1_0, out):
 
         def add1(b):
             t_t[b] = apool.tile([P, 1024], F32, name="t01")
-            nc.vector.tensor_tensor(out=t_t[b][:], in0=s_t[(b, 0)][:], in1=s_t[(b, 1)][:], op=ALU.add)
+            for c in range(2):
+                cols = slice(c * 512, (c + 1) * 512)
+                nc.gpsimd.tensor_tensor(out=t_t[b][:, cols], in0=s_t[(b, 0)][:, cols], in1=s_t[(b, 1)][:, cols], op=ALU.add)
 
         def add2(b):
             a_t[b] = apool.tile([P, 1024], F32, name="a012")
@@ -267,7 +238,7 @@ def tile_equivariantfeedforward_pa_t_kernel(tc, h, x1, pre1, w1_0, b1_0, out):
         def act_takes(b, k):
             if b < 1:
                 return True
-            return k == 3 or k == 1
+            return k == 3
 
         for b in range(4):
             load(b)
@@ -299,11 +270,7 @@ def tile_equivariantfeedforward_pa_t_kernel(tc, h, x1, pre1, w1_0, b1_0, out):
                         quant(n, 2)
                     if ok(n - 2):
                         quant_inv(n - 2)
-                    if ok(t):
-                        sort_out_last_component(t)
                 if g == 1:
-                    if n == NB - 1:
-                        prep_w()
                     if ok(t):
                         evac(t, 0, act_takes(t, 0))
                     if ok(t):
@@ -322,7 +289,7 @@ def tile_equivariantfeedforward_pa_t_kernel(tc, h, x1, pre1, w1_0, b1_0, out):
                         load(next_load)
                         next_load += 1
                     if n == -1:
-                        prep_pre1_second()
+                        prep_w()
                 if n >= NB - 1 and (n, g) != (NB - 1, 0):
                     mm2_bias(next_mm2)
                     next_mm2 += 1

from contextlib import ExitStack

import concourse.mybir as mybir
from concourse.masks import make_identity

FLOPS = 2 * 12288 * 512 * 512 + 2 * 4096 * 1024 * 256

BF16 = mybir.dt.bfloat16
F32 = mybir.dt.float32
U32 = mybir.dt.uint32
U8 = mybir.dt.uint8
FP8X4 = mybir.dt.float8_e4m3fn_x4
AF = mybir.ActivationFunctionType
ALU = mybir.AluOpType

P = 128
NB = 16
BT = 256


def tile_equivariantfeedforward_pa_t_kernel(tc, h, x1, pre1, w1_0, b1_0, out):
    nc = tc.nc

    xv = x1.rearrange("b n (j d) m -> (b n j) (d m)", j=2).rearrange("(g p) c -> p g c", p=P)
    hv = h.rearrange("b n k -> (b n) k").rearrange("(i p) k -> p i k", p=P)
    ov = out.rearrange("b n f -> (b n) f").rearrange("(i p) f -> p i f", p=P)

    with ExitStack() as ctx:
        const = ctx.enter_context(tc.tile_pool(name="const", bufs=1))
        xpool = ctx.enter_context(tc.tile_pool(name="xpool", bufs=4))
        gpool = ctx.enter_context(tc.tile_pool(name="gpool", bufs=2))
        cpool = ctx.enter_context(tc.tile_pool(name="cpool", bufs=3))
        spool = ctx.enter_context(tc.tile_pool(name="spool", bufs=6))
        apool = ctx.enter_context(tc.tile_pool(name="apool", bufs=2))
        vpool = ctx.enter_context(tc.tile_pool(name="vpool", bufs=8))
        ps_tp = ctx.enter_context(tc.psum_pool(name="ps_tp", bufs=3))
        ps_pm = ctx.enter_context(tc.psum_pool(name="ps_pm", bufs=5))
        ctx.enter_context(tc.manual_schedule())

        xs_t, hs_t, tp_t, xg_t, cod_t, scl_t = {}, {}, {}, {}, {}, {}
        pm_t, s_t, t_t, a_t, ig_t, v_t = {}, {}, {}, {}, {}, {}

        ident_bf = const.tile([P, P], BF16, name="ident_bf")
        ident_f = const.tile([P, P], F32, name="ident_f")
        make_identity(nc, ident_bf[:])
        make_identity(nc, ident_f[:])

        one = const.tile([P, 1], F32, name="one")
        one_s = const.tile([P, 1], F32, name="one_s")
        nc.vector.memset(one[:], 1.0)

        pw = const.tile([P, 4, 512], BF16, name="pw")
        pre_v = pre1.rearrange("(j u p) e -> u p j e", j=2, u=2)
        for u in range(2):
            nc.scalar.dma_start(out=pw[:, 2 * u : 2 * u + 2, :], in_=pre_v[u])
        wr = const.tile([P, 2, 4, 256], BF16, name="wr")
        nc.scalar.dma_start(
            out=wr[:, 0].rearrange("p (u e) f -> p u (e f)", u=2),
            in_=w1_0[0:512, :].rearrange("(u p e) f -> p u (e f)", u=2, e=2),
        )
        nc.scalar.dma_start(
            out=wr[:, 1].rearrange("p j f -> p (j f)"),
            in_=w1_0[512:1024, :].rearrange("(p j) f -> p (j f)", j=4),
        )
        bb16 = const.tile([P, 256], BF16, name="bb16")
        nc.scalar.dma_start(out=bb16[:], in_=b1_0.partition_broadcast(P))
        nc.scalar.activation(out=one_s[:], in_=one[:], func=AF.Sqrt)

        pg = const.tile([P, 2048], BF16, name="pg", align_bytes=64)
        pq = const.tile([P, 512], U32, name="pq", align_bytes=64)
        psc = const.tile([P, 512], U8, name="psc", align_bytes=64)
        wg = const.tile([P, 2048], BF16, name="wg", align_bytes=64)
        wq = const.tile([P, 512], U32, name="wq", align_bytes=64)
        wsc = const.tile([P, 512], U8, name="wsc", align_bytes=64)
        bias2 = const.tile([P, 2, 256], F32, name="bias2")
        hq = const.tile([P, NB * BT], U32, name="hq", align_bytes=64)
        hsc = const.tile([P, NB * BT], U8, name="hsc", align_bytes=64)
        iq = const.tile([P, NB * BT], U32, name="iq", align_bytes=64)
        isc = const.tile([P, NB * BT], U8, name="isc", align_bytes=64)

        def prep_pre1():
            nc.vector.tensor_copy(
                out=pg[:].rearrange("p (j q t) -> p j q t", j=4, t=4),
                in_=pw[:].rearrange("p t (q j) -> p j q t", j=4),
            )
            nc.vector.quantize_mx(out=pq[:].bitcast(FP8X4), scales=psc[:], in_=pg[:])

        def prep_w():
            nc.vector.tensor_copy(
                out=wg[:].rearrange("p (s f t) -> p s f t", s=2, t=4),
                in_=wr[:].rearrange("p s t f -> p s f t"),
            )
            nc.vector.quantize_mx(out=wq[:].bitcast(FP8X4), scales=wsc[:], in_=wg[:])
            for i in range(2):
                nc.vector.tensor_copy(out=bias2[:, i, :], in_=bb16[:])

        def load(b):
            xs = xpool.tile([P, 4, 768], BF16, name="xs")
            pieces = 2 if b == 0 else 1
            step = 4 // pieces
            for g in range(0, 4, step):
                nc.sync.dma_start(out=xs[:, g : g + step, :], in_=xv[:, 4 * b + g : 4 * b + g + step, :])
            hs = xpool.tile([P, 2, 512], BF16, name="hs")
            nc.sync.dma_start(out=hs[:], in_=hv[:, 2 * b : 2 * b + 2, :])
            xs_t[b] = xs
            hs_t[b] = hs

        def transposes_h(b):
            th = ps_pm.tile([P, 512], F32, name="pm")
            hw = hs_t[b][:].bitcast(F32)
            for i in range(2):
                for u in range(2):
                    c = 2 * i + u
                    nc.tensor.transpose(th[:, c * P : (c + 1) * P], hw[:, i, u * P : (u + 1) * P], ident_f[:])
            tp_t[(b, 3)] = th

        def transposes_x(b, m):
            tp = ps_tp.tile([P, 1024], BF16, name="tp")
            for g in range(4):
                xg4 = xs_t[b][:, g, :].rearrange("p (u d m) -> p u d m", u=2, m=3)
                for u in range(2):
                    c = 2 * g + u
                    nc.tensor.transpose(tp[:, c * P : (c + 1) * P], xg4[:, u, :, m], ident_bf[:])
            tp_t[(b, m)] = tp

        def evac(b, k, on_act):
            if b not in xg_t:
                xg_t[b] = gpool.tile([P, 4096], BF16, name="xg", align_bytes=64)
            dst = xg_t[b][:, k * 1024 : (k + 1) * 1024].bitcast(F32)
            if k < 3:
                src = tp_t[(b, k)][:].bitcast(F32).rearrange("p (g u a) -> p g a u", g=4, u=2)
                dst = dst.rearrange("p (g a u) -> p g a u", g=4, u=2)
            else:
                src = tp_t[(b, k)][:].rearrange("p (i u t) -> p i t u", i=2, u=2)
                dst = dst.rearrange("p (i t u) -> p i t u", i=2, u=2)
            if on_act:
                nc.scalar.copy(out=dst, in_=src)
            else:
                nc.vector.tensor_copy(out=dst, in_=src)

        def quant(b, k):
            grouped = xg_t[b][:, k * 1024 : (k + 1) * 1024]
            if k == 3:
                cols = slice(b * BT, (b + 1) * BT)
                nc.vector.quantize_mx(out=hq[:, cols].bitcast(FP8X4), scales=hsc[:, cols], in_=grouped)
                return
            if b not in cod_t:
                cod_t[b] = cpool.tile([P, 768], U32, name="cod", align_bytes=64)
                scl_t[b] = cpool.tile([P, 768], U8, name="scl", align_bytes=64)
            cols = slice(k * BT, (k + 1) * BT)
            nc.vector.quantize_mx(out=cod_t[b][:, cols].bitcast(FP8X4), scales=scl_t[b][:, cols], in_=grouped)

        def mm1(b, m, jp):
            pm = ps_pm.tile([P, 512], F32, name="pm")
            for j2 in range(2):
                j = 2 * jp + j2
                nc.tensor.matmul_mx(
                    out=pm[:, j2 * BT : (j2 + 1) * BT],
                    lhsT=pq[:, j * P : (j + 1) * P].bitcast(FP8X4),
                    lhsT_scale=psc[:, j * P : (j + 1) * P],
                    rhs=cod_t[b][:, m * BT : (m + 1) * BT].bitcast(FP8X4),
                    rhs_scale=scl_t[b][:, m * BT : (m + 1) * BT],
                    start=True,
                    stop=True,
                )
            pm_t[(b, m, jp)] = pm

        def square(b, m, jp):
            if jp == 0:
                s_t[(b, m)] = spool.tile([P, 1024], F32, name="sq")
            nc.scalar.activation(out=s_t[(b, m)][:, jp * 512 : (jp + 1) * 512], in_=pm_t[(b, m, jp)][:], func=AF.Square)

        def add1(b):
            t_t[b] = apool.tile([P, 1024], F32, name="t01")
            for c in range(2):
                cols = slice(c * 512, (c + 1) * 512)
                nc.gpsimd.tensor_tensor(out=t_t[b][:, cols], in0=s_t[(b, 0)][:, cols], in1=s_t[(b, 1)][:, cols], op=ALU.add)

        def add2(b):
            a_t[b] = apool.tile([P, 1024], F32, name="a012")
            nc.vector.tensor_tensor(
                out=a_t[b][:].rearrange("p (c t j) -> p c t j", c=2, j=2),
                in0=t_t[b][:].rearrange("p (c j t) -> p c t j", c=2, j=2),
                in1=s_t[(b, 2)][:].rearrange("p (c j t) -> p c t j", c=2, j=2),
                op=ALU.add,
            )

        def root(b):
            ig_t[b] = apool.tile([P, 1024], BF16, name="ig", align_bytes=64)
            nc.scalar.activation(
                out=ig_t[b][:].rearrange("p (t c j) -> p t c j", c=2, j=2),
                in_=a_t[b][:].rearrange("p (c t j) -> p t c j", c=2, j=2),
                func=AF.Sqrt,
            )

        def quant_inv(b):
            cols = slice(b * BT, (b + 1) * BT)
            nc.vector.quantize_mx(out=iq[:, cols].bitcast(FP8X4), scales=isc[:, cols], in_=ig_t[b][:])

        def mm2_bias(b):
            ob = ps_pm.tile([P, 512], F32, name="pm")
            for i in range(2):
                o = ob[:, i * 256 : (i + 1) * 256]
                cols = slice(b * BT + i * P, b * BT + (i + 1) * P)
                nc.tensor.matmul_mx(
                    out=o,
                    lhsT=hq[:, cols].bitcast(FP8X4),
                    lhsT_scale=hsc[:, cols],
                    rhs=wq[:, 0:256].bitcast(FP8X4),
                    rhs_scale=wsc[:, 0:256],
                    start=True,
                    stop=False,
                )
                nc.tensor.matmul_mx(
                    out=o,
                    lhsT=iq[:, cols].bitcast(FP8X4),
                    lhsT_scale=isc[:, cols],
                    rhs=wq[:, 256:512].bitcast(FP8X4),
                    rhs_scale=wsc[:, 256:512],
                    start=False,
                    stop=True,
                )
            v_t[b] = vpool.tile([P, 512], F32, name="v")
            nc.vector.tensor_tensor(
                out=v_t[b][:],
                in0=ob[:],
                in1=bias2[:].rearrange("p i f -> p (i f)"),
                op=ALU.add,
            )

        def silu_store(b):
            nc.scalar.activation(out=v_t[b][:], in_=v_t[b][:], func=AF.Silu)
            nc.sync.dma_start(out=ov[:, 2 * b : 2 * b + 2, :], in_=v_t[b][:].rearrange("p (i f) -> p i f", i=2))

        def ok(b):
            return 0 <= b < NB

        def act_takes(b, k):
            if b < 1:
                return True
            return k == 3

        for b in range(4):
            load(b)
        next_load = 4
        prep_pre1()

        next_mm2 = 0
        for n in range(-1, NB + 2):
            t = n + 1
            for g in range(3):
                if ok(n):
                    for jp in range(2):
                        mm1(n, g, jp)
                if ok(t):
                    transposes_x(t, g)
                    if g == 0:
                        transposes_h(t)
                if ok(n):
                    for jp in range(2):
                        square(n, g, jp)
                if g == 0:
                    if ok(n):
                        evac(n, 2, act_takes(n, 2))
                    if ok(t):
                        evac(t, 3, act_takes(t, 3))
                    if ok(n - 1):
                        add2(n - 1)
                    if ok(n):
                        quant(n, 2)
                    if ok(n - 2):
                        quant_inv(n - 2)
                if g == 1:
                    if ok(t):
                        evac(t, 0, act_takes(t, 0))
                    if ok(t):
                        quant(t, 3)
                        quant(t, 0)
                if g == 2:
                    if ok(t):
                        evac(t, 1, act_takes(t, 1))
                    if ok(n - 1):
                        root(n - 1)
                    if ok(n):
                        add1(n)
                    if ok(t):
                        quant(t, 1)
                    if ok(t) and next_load < NB:
                        load(next_load)
                        next_load += 1
                    if n == -1:
                        prep_w()
                if n >= NB - 1 and (n, g) != (NB - 1, 0):
                    mm2_bias(next_mm2)
                    next_mm2 += 1
        for b in range(NB):
            while next_mm2 < min(NB, b + 4):
                mm2_bias(next_mm2)
                next_mm2 += 1
            silu_store(b)
